import numpy as np
import ml_dtypes


def mxq(x, axis, fmt="e4m3"):
    dtype, down = {"e4m3": (ml_dtypes.float8_e4m3fn, 7), "e5m2": (ml_dtypes.float8_e5m2, 14)}[fmt]
    v = np.moveaxis(np.asarray(x, np.float32).astype(ml_dtypes.bfloat16).astype(np.float64), axis, -1)
    blocks = v.reshape(v.shape[:-1] + (-1, 32))
    amax = np.abs(blocks).max(-1, keepdims=True)
    byte = np.maximum(np.where(amax > 0, np.frexp(amax)[1] - 1 + 127, 0) - down, 1)
    scale = np.exp2(byte - 127.0)
    codes = (blocks / scale).astype(np.float32).astype(dtype).astype(np.float64)
    return np.moveaxis((codes * scale).reshape(v.shape), -1, axis)


WIDE = False


def mx_kscale(k):
    if not WIDE:
        return np.ones(k)
    levels = np.array([10, -10, 5, -5, 0])
    a = np.random.permutation(np.resize(levels, k // 512 * 4)).reshape(k // 512, 4)
    idx = np.arange(k)
    return np.exp2(a[idx // 512, idx % 128 // 32])


BF16 = ml_dtypes.bfloat16


def bf(x):
    return np.asarray(x, np.float32).astype(BF16)


def f64(x):
    return np.asarray(x).astype(np.float64)


E2M1 = np.array([0.0, 0.5, 1.0, 1.5, 2.0, 3.0, 4.0, 6.0, -0.0, -0.5, -1.0, -1.5, -2.0, -3.0, -4.0, -6.0])


def pack_weight(w, fmt):
    k, n = w.shape
    w = f64(bf(w)).reshape(k // 32, 32, n)
    amax = np.abs(w).max(1)
    if fmt == "e4m3":
        byte = np.frexp(amax)[1] - 1 + 127 - 7
    else:
        mant, ex = np.frexp(amax / 6.0)
        byte = np.where(mant > 0.5, ex, ex - 1) + 127
    byte = np.clip(np.where(amax > 0, byte, 1), 1, 254)
    scaled = (w * np.exp2(127.0 - byte)[:, None, :]).reshape(k, n).astype(np.float32)
    by_word = np.ascontiguousarray(scaled.reshape(k // 512, 128, 4, n).transpose(0, 1, 3, 2))
    if fmt == "e4m3":
        words = by_word.astype(ml_dtypes.float8_e4m3fn).view(np.uint8)
    else:
        c = by_word.astype(ml_dtypes.float4_e2m1fn).view(np.uint8) & 0xF
        words = c[..., 0::2] | (c[..., 1::2] << 4)
    return np.ascontiguousarray(words), np.ascontiguousarray(byte.astype(np.uint8).reshape(k // 512, 16, n))


def unpack_weight(words, scales, fmt):
    g, p, n, _ = words.shape
    if fmt == "e4m3":
        vals = np.ascontiguousarray(words).view(ml_dtypes.float8_e4m3fn).astype(np.float64)
    else:
        nib = np.empty((g, p, n, 4), np.uint8)
        nib[..., 0::2] = words & 0xF
        nib[..., 1::2] = words >> 4
        vals = E2M1[nib]
    vals = vals * np.repeat(np.exp2(scales.astype(np.float64) - 127.0), 8, axis=1)[..., None]
    return vals.transpose(0, 1, 3, 2).reshape(g * 512, n)


B, C, O, H, W, P, Q = 4, 512, 512, 16, 16, 5, 4
PMAX = max(P, Q)
HW = H * W


def order_rms(n):
    return np.sqrt(np.array([np.prod(np.arange(1.0, 2.0 * i, 2.0)) for i in range(1, n + 1)]))[:, None, None]


def kpow(s, n):
    return np.exp2(np.log2(s)[None, None, :] * np.arange(1, n + 1)[:, None, None])


def setup_inputs():
    s = mx_kscale(C)
    x = bf(np.random.standard_normal((B, C, H, W)) * s[None, :, None, None])
    Wp = np.random.standard_normal((P, O, C)) / (np.sqrt(C) * order_rms(P)) / kpow(s, P)
    bp = bf(np.random.standard_normal(O) * 0.5)
    Wq = np.random.standard_normal((Q, O, C)) / (np.sqrt(C) * order_rms(Q)) / kpow(s, Q)
    Wp_words, Wp_scales = pack_weight(np.ascontiguousarray(Wp.swapaxes(1, 2)).reshape(-1, O), "e4m3")
    Wq_words, Wq_scales = pack_weight(np.ascontiguousarray(Wq.swapaxes(1, 2)).reshape(-1, O), "e4m3")
    return {"x": x,
            "Wp_words": Wp_words, "Wp_scales": Wp_scales,
            "bp": bp,
            "Wq_words": Wq_words, "Wq_scales": Wq_scales}


def reference(x, Wp_words, Wp_scales, bp, Wq_words, Wq_scales):
    x = f64(x)
    pows = [x]
    for _ in range(PMAX - 1):
        pows.append(pows[-1] * x)
    Xs = np.stack(pows, axis=0)
    Xr = Xs.reshape(PMAX, B, C, HW).transpose(1, 3, 0, 2).reshape(B * HW, PMAX * C)
    Xq = mxq(Xr, 1, "e4m3")
    Wpq = unpack_weight(Wp_words, Wp_scales, "e4m3").reshape(P, C, O).reshape(P * C, O)
    Wqq = unpack_weight(Wq_words, Wq_scales, "e4m3").reshape(Q, C, O).reshape(Q * C, O)
    sum_p = (Xq[:, :P * C] @ Wpq) + f64(bp)[None, :]
    sum_q = Xq[:, :Q * C] @ Wqq
    out = sum_p / (1.0 + np.abs(sum_q))
    return np.ascontiguousarray(out.reshape(B, H, W, O).transpose(0, 3, 1, 2))

@@ -1,0 +1,187 @@
+from contextlib import ExitStack
+
+import concourse.mybir as mybir
+from concourse.masks import make_identity
+
+BF16 = mybir.dt.bfloat16
+F32 = mybir.dt.float32
+I32 = mybir.dt.int32
+U32 = mybir.dt.uint32
+U8 = mybir.dt.uint8
+FP8X4 = mybir.dt.float8_e4m3fn_x4
+ACT = mybir.ActivationFunctionType
+ALU = mybir.AluOpType
+
+P = 128
+PACK = 4
+CHUNKS, CHANNELS, PIXELS, OUT_CH = 4, 512, 256, 512
+ORDERS_P, ORDERS_Q = 5, 4
+WIDTH = PIXELS * PACK
+M_TILES = OUT_CH // P
+PAIRS = M_TILES // 2
+RUN = 4
+SCALAR_ROUNDS_X4 = CHUNKS // 2
+FINISH_LAG = 3
+
+FLOPS = 2 * CHUNKS * PIXELS * OUT_CH * CHANNELS * (ORDERS_P + ORDERS_Q)
+
+
+def load_scale_planes(nc, planes, scales_in):
+    by_row = scales_in.rearrange("g (quad r) n -> r quad g n", r=4)
+    for r in range(4):
+        nc.sync.dma_start(out=planes[r:P:32, :, :].bitcast(I32), in_=by_row[r].bitcast(I32))
+
+
+def tile_kanvolutionlayer_e_kernel(tc, x, Wp_words, Wp_scales, bp, Wq_words, Wq_scales, out):
+    nc = tc.nc
+    with ExitStack() as ctx:
+        ctx.enter_context(tc.manual_schedule())
+        keep = ctx.enter_context(tc.tile_pool(name="keep", bufs=1))
+        powers = ctx.enter_context(tc.tile_pool(name="powers", bufs=3))
+        scratch = ctx.enter_context(tc.tile_pool(name="scratch", bufs=2))
+        recips = ctx.enter_context(tc.tile_pool(name="recips", bufs=2 * FINISH_LAG))
+        results = ctx.enter_context(tc.tile_pool(name="results", bufs=3))
+        banks = ctx.enter_context(tc.psum_pool(name="banks", bufs=2 * PAIRS))
+
+        x_raw = keep.tile([P, CHUNKS, WIDTH], BF16, name="x_raw")
+
+        def load_x(queue, c):
+            queue.dma_start(out=x_raw[:, c, :], in_=x[c].rearrange("(p t) h w -> p (t h w)", t=PACK))
+
+        words_q = keep.tile([P, ORDERS_Q, PACK * OUT_CH], U8, name="words_q", align_bytes=64)
+        words_p = keep.tile([P, ORDERS_P, PACK * OUT_CH], U8, name="words_p", align_bytes=64)
+        planes_q = keep.tile([P, ORDERS_Q, OUT_CH], U8, name="planes_q", align_bytes=64)
+        planes_p = keep.tile([P, ORDERS_P, OUT_CH], U8, name="planes_p", align_bytes=64)
+        bias_rows = keep.tile([P, P], BF16, name="bias_rows")
+        one = keep.tile([P, 1], F32, name="one")
+        nc.vector.memset(planes_q[:].bitcast(I32), 0)
+        nc.vector.memset(planes_p[:].bitcast(I32), 0)
+        nc.vector.memset(bias_rows[:], 0.0)
+        nc.vector.memset(one[:], 1.0)
+
+        load_x(nc.scalar, 0)
+        load_x(nc.scalar, 1)
+        nc.scalar.dma_start(out=bias_rows[0:M_TILES, :], in_=bp.rearrange("(m p) -> m p", p=P))
+        nc.sync.dma_start(out=words_q[:].bitcast(I32), in_=Wq_words.rearrange("g p n t -> p g (n t)").bitcast(I32))
+        load_scale_planes(nc, planes_q, Wq_scales)
+        load_scale_planes(nc, planes_p, Wp_scales)
+        load_x(nc.sync, 2)
+        nc.sync.dma_start(out=words_p[:].bitcast(I32), in_=Wp_words.rearrange("g p n t -> p g (n t)").bitcast(I32))
+        load_x(nc.sync, 3)
+
+        warm = keep.tile([P, 1], F32, name="warm")
+        nc.scalar.activation(out=warm[:], in_=one[:], func=ACT.Abs_reciprocal_sqrt)
+
+        ident = keep.tile([P, P], BF16, name="ident")
+        make_identity(nc, ident[:])
+        bias_ps = banks.tile([P, P], BF16, name="bias_ps", tag="sum_q")
+        nc.tensor.transpose(bias_ps[:], bias_rows[:], ident[:])
+        bias_col = keep.tile([P, M_TILES], F32, name="bias_col")
+
+        codes = keep.tile([P, ORDERS_P, CHUNKS * PIXELS], U32, name="codes", align_bytes=64)
+        x_planes = keep.tile([P, ORDERS_P, CHUNKS * PIXELS], U8, name="x_planes", align_bytes=64)
+        x1, x2_f32, x4_f32, x4 = {}, {}, {}, {}
+        sum_q, sum_p, recip = {}, {}, {}
+
+        def quantise(order, c, values):
+            cols = slice(c * PIXELS, (c + 1) * PIXELS)
+            nc.vector.quantize_mx(
+                out=codes[:, order, cols].bitcast(FP8X4), scales=x_planes[:, order, cols], in_=values
+            )
+
+        def powers_1_and_2(c):
+            x1[c] = powers.tile([P, WIDTH], BF16, name="x1", align_bytes=64)
+            nc.vector.tensor_copy(
+                out=x1[c][:].rearrange("p (g i t) -> p g t i", i=RUN, t=PACK),
+                in_=x_raw[:, c, :].rearrange("p (t g i) -> p g t i", t=PACK, i=RUN),
+            )
+            x2 = powers.tile([P, WIDTH], BF16, name="x2", align_bytes=64)
+            nc.vector.tensor_tensor(out=x2[:], in0=x1[c][:], in1=x1[c][:], op=ALU.mult)
+            quantise(0, c, x1[c][:])
+            quantise(1, c, x2[:])
+
+        def even_powers_in_float32(c):
+            x2_f32[c] = powers.tile([P, WIDTH], F32, name="x2_f32")
+            nc.scalar.activation(out=x2_f32[c][:], in_=x1[c][:], func=ACT.Square)
+            x4_f32[c] = powers.tile([P, WIDTH], F32, name="x4_f32")
+            nc.scalar.activation(out=x4_f32[c][:], in_=x2_f32[c][:], func=ACT.Square)
+            x4[c] = powers.tile([P, WIDTH], BF16, name="x4", align_bytes=64)
+            if c < SCALAR_ROUNDS_X4:
+                nc.scalar.activation(out=x4[c][:], in_=x2_f32[c][:], func=ACT.Square)
+
+        def powers_3_to_5(c):
+            x3 = powers.tile([P, WIDTH], BF16, name="x3", align_bytes=64)
+            nc.vector.tensor_tensor(out=x3[:], in0=x2_f32[c][:], in1=x1[c][:], op=ALU.mult)
+            if c >= SCALAR_ROUNDS_X4:
+                nc.vector.tensor_copy(out=x4[c][:], in_=x4_f32[c][:])
+            quantise(2, c, x3[:])
+            quantise(3, c, x4[c][:])
+            x5 = powers.tile([P, WIDTH], BF16, name="x5", align_bytes=64)
+            nc.vector.tensor_tensor(out=x5[:], in0=x4_f32[c][:], in1=x1[c][:], op=ALU.mult)
+            return x5
+
+        def contract(c, sums, tag, words, planes, orders):
+            cols = slice(c * PIXELS, (c + 1) * PIXELS)
+            for pair in range(PAIRS):
+                sums[(c, pair)] = banks.tile([P, 2, PIXELS], F32, name=tag, tag=tag)
+                for j in range(2):
+                    m = 2 * pair + j
+                    for order in range(orders):
+                        nc.tensor.matmul_mx(
+                            out=sums[(c, pair)][:, j, :],
+                            lhsT=words[:, order, m * PACK * P : (m + 1) * PACK * P].bitcast(FP8X4),
+                            lhsT_scale=planes[:, order, m * P : (m + 1) * P],
+                            rhs=codes[:, order, cols].bitcast(FP8X4),
+                            rhs_scale=x_planes[:, order, cols],
+                            start=(order == 0),
+                            stop=(order == orders - 1),
+                        )
+
+        def reciprocals(c):
+            mag, rsqrt = {}, {}
+            for pair in range(PAIRS):
+                mag[pair] = scratch.tile([P, 2, PIXELS], F32, name="mag")
+                nc.scalar.activation(out=mag[pair][:], in_=sum_q[(c, pair)][:], func=ACT.Abs)
+            for pair in range(PAIRS):
+                rsqrt[pair] = scratch.tile([P, 2, PIXELS], F32, name="rsqrt")
+                nc.scalar.activation(out=rsqrt[pair][:], in_=mag[pair][:], func=ACT.Abs_reciprocal_sqrt, bias=1.0)
+            for pair in range(PAIRS):
+                recip[(c, pair)] = recips.tile([P, 2, PIXELS], F32, name="recip")
+                nc.scalar.activation(out=recip[(c, pair)][:], in_=rsqrt[pair][:], func=ACT.Square)
+
+        def finish(c, pair):
+            res = results.tile([P, 2, PIXELS], F32, name="res")
+            for j in range(2):
+                m = 2 * pair + j
+                nc.vector.scalar_tensor_tensor(
+                    out=res[:, j, :],
+                    in0=sum_p[(c, pair)][:, j, :],
+                    scalar=bias_col[:, m : m + 1],
+                    in1=recip[(c, pair)][:, j, :],
+                    op0=ALU.add,
+                    op1=ALU.mult,
+                )
+            nc.sync.dma_start(
+                out=out[c, 2 * pair * P : 2 * (pair + 1) * P].rearrange("(j o) h w -> o j (h w)", j=2), in_=res[:]
+            )
+
+        for step in range(CHUNKS + FINISH_LAG):
+            middle = step - 1
+            last = step - FINISH_LAG
+            if step < CHUNKS:
+                powers_1_and_2(step)
+                even_powers_in_float32(step)
+            if step == 0:
+                nc.vector.tensor_copy(out=bias_col[:], in_=bias_ps[:, 0:M_TILES])
+            if 0 <= middle < CHUNKS:
+                x5 = powers_3_to_5(middle)
+            if last >= 0:
+                finish(last, 0)
+            if 0 <= middle < CHUNKS:
+                quantise(4, middle, x5[:])
+            if last >= 0:
+                finish(last, 1)
+            if 0 <= middle < CHUNKS:
+                contract(middle, sum_q, "sum_q", words_q, planes_q, ORDERS_Q)
+                contract(middle, sum_p, "sum_p", words_p, planes_p, ORDERS_P)
+                reciprocals(middle)

@@ -21,7 +21,7 @@ M_TILES = OUT_CH // P
 PAIRS = M_TILES // 2
 RUN = 4
 SCALAR_ROUNDS_X4 = CHUNKS // 2
-FINISH_LAG = 3
+FINISH_LAG = 4
 
 FLOPS = 2 * CHUNKS * PIXELS * OUT_CH * CHANNELS * (ORDERS_P + ORDERS_Q)
 
@@ -38,10 +38,11 @@ def tile_kanvolutionlayer_e_kernel(tc, x, Wp_words, Wp_scales, bp, Wq_words, Wq_
         ctx.enter_context(tc.manual_schedule())
         keep = ctx.enter_context(tc.tile_pool(name="keep", bufs=1))
         powers = ctx.enter_context(tc.tile_pool(name="powers", bufs=3))
-        scratch = ctx.enter_context(tc.tile_pool(name="scratch", bufs=2))
-        recips = ctx.enter_context(tc.tile_pool(name="recips", bufs=2 * FINISH_LAG))
+        scratch = ctx.enter_context(tc.tile_pool(name="scratch", bufs=2 * PAIRS))
+        recips = ctx.enter_context(tc.tile_pool(name="recips", bufs=PAIRS * (FINISH_LAG - 1)))
         results = ctx.enter_context(tc.tile_pool(name="results", bufs=3))
-        banks = ctx.enter_context(tc.psum_pool(name="banks", bufs=2 * PAIRS))
+        q_banks = ctx.enter_context(tc.psum_pool(name="q_banks", bufs=PAIRS))
+        p_banks = ctx.enter_context(tc.psum_pool(name="p_banks", bufs=PAIRS * (FINISH_LAG - 1)))
 
         x_raw = keep.tile([P, CHUNKS, WIDTH], BF16, name="x_raw")
 
@@ -74,80 +75,80 @@ def tile_kanvolutionlayer_e_kernel(tc, x, Wp_words, Wp_scales, bp, Wq_words, Wq_
 
         ident = keep.tile([P, P], BF16, name="ident")
         make_identity(nc, ident[:])
-        bias_ps = banks.tile([P, P], BF16, name="bias_ps", tag="sum_q")
+        bias_ps = q_banks.tile([P, P], BF16, name="bias_ps", tag="sum_q")
         nc.tensor.transpose(bias_ps[:], bias_rows[:], ident[:])
         bias_col = keep.tile([P, M_TILES], F32, name="bias_col")
 
         codes = keep.tile([P, ORDERS_P, CHUNKS * PIXELS], U32, name="codes", align_bytes=64)
         x_planes = keep.tile([P, ORDERS_P, CHUNKS * PIXELS], U8, name="x_planes", align_bytes=64)
-        x1, x2_f32, x4_f32, x4 = {}, {}, {}, {}
-        sum_q, sum_p, recip = {}, {}, {}
+        power = {}
+        x2_f32, x4_f32 = {}, {}
+        sum_q, sum_p, rsqrt, recip = {}, {}, {}, {}
 
-        def quantise(order, c, values):
+        def new_power(order, c):
+            power[(order, c)] = powers.tile([P, WIDTH], BF16, name="x%d" % order, align_bytes=64)
+            return power[(order, c)]
+
+        def quantise(order, c):
             cols = slice(c * PIXELS, (c + 1) * PIXELS)
             nc.vector.quantize_mx(
-                out=codes[:, order, cols].bitcast(FP8X4), scales=x_planes[:, order, cols], in_=values
+                out=codes[:, order - 1, cols].bitcast(FP8X4),
+                scales=x_planes[:, order - 1, cols],
+                in_=power[(order, c)][:],
             )
 
-        def powers_1_and_2(c):
-            x1[c] = powers.tile([P, WIDTH], BF16, name="x1", align_bytes=64)
+        def regroup_x(c):
             nc.vector.tensor_copy(
-                out=x1[c][:].rearrange("p (g i t) -> p g t i", i=RUN, t=PACK),
+                out=new_power(1, c)[:].rearrange("p (g i t) -> p g t i", i=RUN, t=PACK),
                 in_=x_raw[:, c, :].rearrange("p (t g i) -> p g t i", t=PACK, i=RUN),
             )
-            x2 = powers.tile([P, WIDTH], BF16, name="x2", align_bytes=64)
-            nc.vector.tensor_tensor(out=x2[:], in0=x1[c][:], in1=x1[c][:], op=ALU.mult)
-            quantise(0, c, x1[c][:])
-            quantise(1, c, x2[:])
 
-        def even_powers_in_float32(c):
-            x2_f32[c] = powers.tile([P, WIDTH], F32, name="x2_f32")
-            nc.scalar.activation(out=x2_f32[c][:], in_=x1[c][:], func=ACT.Square)
-            x4_f32[c] = powers.tile([P, WIDTH], F32, name="x4_f32")
-            nc.scalar.activation(out=x4_f32[c][:], in_=x2_f32[c][:], func=ACT.Square)
-            x4[c] = powers.tile([P, WIDTH], BF16, name="x4", align_bytes=64)
-            if c < SCALAR_ROUNDS_X4:
-                nc.scalar.activation(out=x4[c][:], in_=x2_f32[c][:], func=ACT.Square)
+        def times_x(order, c, lower_power):
+            nc.vector.tensor_tensor(out=new_power(order, c)[:], in0=lower_power[:], in1=power[(1, c)][:], op=ALU.mult)
 
-        def powers_3_to_5(c):
-            x3 = powers.tile([P, WIDTH], BF16, name="x3", align_bytes=64)
-            nc.vector.tensor_tensor(out=x3[:], in0=x2_f32[c][:], in1=x1[c][:], op=ALU.mult)
+        def round_x4_on_vector(c):
             if c >= SCALAR_ROUNDS_X4:
-                nc.vector.tensor_copy(out=x4[c][:], in_=x4_f32[c][:])
-            quantise(2, c, x3[:])
-            quantise(3, c, x4[c][:])
-            x5 = powers.tile([P, WIDTH], BF16, name="x5", align_bytes=64)
-            nc.vector.tensor_tensor(out=x5[:], in0=x4_f32[c][:], in1=x1[c][:], op=ALU.mult)
-            return x5
+                nc.vector.tensor_copy(out=new_power(4, c)[:], in_=x4_f32[c][:])
 
-        def contract(c, sums, tag, words, planes, orders):
+        def square_to_float32(squares, name, c, values):
+            squares[c] = powers.tile([P, WIDTH], F32, name=name)
+            nc.scalar.activation(out=squares[c][:], in_=values[:], func=ACT.Square)
+
+        def round_x4_on_scalar(c):
+            if c < SCALAR_ROUNDS_X4:
+                nc.scalar.activation(out=new_power(4, c)[:], in_=x2_f32[c][:], func=ACT.Square)
+
+        def contract(c, sums, banks, tag, words, planes, orders):
             cols = slice(c * PIXELS, (c + 1) * PIXELS)
             for pair in range(PAIRS):
                 sums[(c, pair)] = banks.tile([P, 2, PIXELS], F32, name=tag, tag=tag)
                 for j in range(2):
                     m = 2 * pair + j
-                    for order in range(orders):
+                    for g in range(orders):
                         nc.tensor.matmul_mx(
                             out=sums[(c, pair)][:, j, :],
-                            lhsT=words[:, order, m * PACK * P : (m + 1) * PACK * P].bitcast(FP8X4),
-                            lhsT_scale=planes[:, order, m * P : (m + 1) * P],
-                            rhs=codes[:, order, cols].bitcast(FP8X4),
-                            rhs_scale=x_planes[:, order, cols],
-                            start=(order == 0),
-                            stop=(order == orders - 1),
+                            lhsT=words[:, g, m * PACK * P : (m + 1) * PACK * P].bitcast(FP8X4),
+                            lhsT_scale=planes[:, g, m * P : (m + 1) * P],
+                            rhs=codes[:, g, cols].bitcast(FP8X4),
+                            rhs_scale=x_planes[:, g, cols],
+                            start=(g == 0),
+                            stop=(g == orders - 1),
                         )
 
-        def reciprocals(c):
-            mag, rsqrt = {}, {}
+        def reciprocal_roots(c):
+            mag = {}
             for pair in range(PAIRS):
                 mag[pair] = scratch.tile([P, 2, PIXELS], F32, name="mag")
                 nc.scalar.activation(out=mag[pair][:], in_=sum_q[(c, pair)][:], func=ACT.Abs)
             for pair in range(PAIRS):
-                rsqrt[pair] = scratch.tile([P, 2, PIXELS], F32, name="rsqrt")
-                nc.scalar.activation(out=rsqrt[pair][:], in_=mag[pair][:], func=ACT.Abs_reciprocal_sqrt, bias=1.0)
-            for pair in range(PAIRS):
-                recip[(c, pair)] = recips.tile([P, 2, PIXELS], F32, name="recip")
-                nc.scalar.activation(out=recip[(c, pair)][:], in_=rsqrt[pair][:], func=ACT.Square)
+                rsqrt[(c, pair)] = scratch.tile([P, 2, PIXELS], F32, name="rsqrt")
+                nc.scalar.activation(
+                    out=rsqrt[(c, pair)][:], in_=mag[pair][:], func=ACT.Abs_reciprocal_sqrt, bias=1.0
+                )
+
+        def reciprocal(c, pair):
+            recip[(c, pair)] = recips.tile([P, 2, PIXELS], F32, name="recip")
+            nc.scalar.activation(out=recip[(c, pair)][:], in_=rsqrt[(c, pair)][:], func=ACT.Square)
 
         def finish(c, pair):
             res = results.tile([P, 2, PIXELS], F32, name="res")
@@ -165,23 +166,44 @@ def tile_kanvolutionlayer_e_kernel(tc, x, Wp_words, Wp_scales, bp, Wq_words, Wq_
                 out=out[c, 2 * pair * P : 2 * (pair + 1) * P].rearrange("(j o) h w -> o j (h w)", j=2), in_=res[:]
             )
 
+        def live(c):
+            return 0 <= c < CHUNKS
+
         for step in range(CHUNKS + FINISH_LAG):
-            middle = step - 1
-            last = step - FINISH_LAG
-            if step < CHUNKS:
-                powers_1_and_2(step)
-                even_powers_in_float32(step)
+            new, mid, old, done = step, step - 1, step - 2, step - FINISH_LAG
+            if live(mid):
+                times_x(3, mid, x2_f32[mid])
+            if live(new):
+                regroup_x(new)
+            if live(mid):
+                round_x4_on_vector(mid)
+                quantise(3, mid)
+                quantise(4, mid)
+                times_x(5, mid, x4_f32[mid])
+            if live(new):
+                times_x(2, new, power[(1, new)])
+            if live(done):
+                finish(done, 0)
+            if live(mid):
+                quantise(5, mid)
+            if live(new):
+                quantise(1, new)
+                quantise(2, new)
+            if live(done):
+                finish(done, 1)
             if step == 0:
                 nc.vector.tensor_copy(out=bias_col[:], in_=bias_ps[:, 0:M_TILES])
-            if 0 <= middle < CHUNKS:
-                x5 = powers_3_to_5(middle)
-            if last >= 0:
-                finish(last, 0)
-            if 0 <= middle < CHUNKS:
-                quantise(4, middle, x5[:])
-            if last >= 0:
-                finish(last, 1)
-            if 0 <= middle < CHUNKS:
-                contract(middle, sum_q, "sum_q", words_q, planes_q, ORDERS_Q)
-                contract(middle, sum_p, "sum_p", words_p, planes_p, ORDERS_P)
-                reciprocals(middle)
+            if live(new):
+                square_to_float32(x2_f32, "x2_f32", new, power[(1, new)])
+            if live(old):
+                reciprocal(old, 0)
+            if live(new):
+                square_to_float32(x4_f32, "x4_f32", new, x2_f32[new])
+            if live(old):
+                reciprocal(old, 1)
+            if live(new):
+                round_x4_on_scalar(new)
+            if live(mid):
+                contract(mid, sum_q, q_banks, "sum_q", words_q, planes_q, ORDERS_Q)
+                contract(mid, sum_p, p_banks, "sum_p", words_p, planes_p, ORDERS_P)
+                reciprocal_roots(mid)

@@ -60,8 +60,8 @@ def tile_kanvolutionlayer_e_kernel(tc, x, Wp_words, Wp_scales, bp, Wq_words, Wq_
         nc.vector.memset(bias_rows[:], 0.0)
         nc.vector.memset(one[:], 1.0)
 
-        load_x(nc.scalar, 0)
-        load_x(nc.scalar, 1)
+        load_x(nc.sync, 0)
+        load_x(nc.sync, 1)
         nc.scalar.dma_start(out=bias_rows[0:M_TILES, :], in_=bp.rearrange("(m p) -> m p", p=P))
         nc.sync.dma_start(out=words_q[:].bitcast(I32), in_=Wq_words.rearrange("g p n t -> p g (n t)").bitcast(I32))
         load_scale_planes(nc, planes_q, Wq_scales)

@@ -40,7 +40,7 @@ def tile_kanvolutionlayer_e_kernel(tc, x, Wp_words, Wp_scales, bp, Wq_words, Wq_
         powers = ctx.enter_context(tc.tile_pool(name="powers", bufs=3))
         scratch = ctx.enter_context(tc.tile_pool(name="scratch", bufs=2 * PAIRS))
         recips = ctx.enter_context(tc.tile_pool(name="recips", bufs=PAIRS * (FINISH_LAG - 1)))
-        results = ctx.enter_context(tc.tile_pool(name="results", bufs=3))
+        results = ctx.enter_context(tc.tile_pool(name="results", bufs=4))
         q_banks = ctx.enter_context(tc.psum_pool(name="q_banks", bufs=PAIRS))
         p_banks = ctx.enter_context(tc.psum_pool(name="p_banks", bufs=PAIRS * (FINISH_LAG - 1)))
 
@@ -151,20 +151,18 @@ def tile_kanvolutionlayer_e_kernel(tc, x, Wp_words, Wp_scales, bp, Wq_words, Wq_
             nc.scalar.activation(out=recip[(c, pair)][:], in_=rsqrt[(c, pair)][:], func=ACT.Square)
 
         def finish(c, pair):
-            res = results.tile([P, 2, PIXELS], F32, name="res")
             for j in range(2):
                 m = 2 * pair + j
+                res = results.tile([P, PIXELS], F32, name="res")
                 nc.vector.scalar_tensor_tensor(
-                    out=res[:, j, :],
+                    out=res[:],
                     in0=sum_p[(c, pair)][:, j, :],
                     scalar=bias_col[:, m : m + 1],
                     in1=recip[(c, pair)][:, j, :],
                     op0=ALU.add,
                     op1=ALU.mult,
                 )
-            nc.sync.dma_start(
-                out=out[c, 2 * pair * P : 2 * (pair + 1) * P].rearrange("(j o) h w -> o j (h w)", j=2), in_=res[:]
-            )
+                nc.sync.dma_start(out=out[c, m * P : (m + 1) * P].rearrange("o h w -> o (h w)"), in_=res[:])
 
         def live(c):
             return 0 <= c < CHUNKS
@@ -175,6 +173,8 @@ def tile_kanvolutionlayer_e_kernel(tc, x, Wp_words, Wp_scales, bp, Wq_words, Wq_
                 times_x(3, mid, x2_f32[mid])
             if live(new):
                 regroup_x(new)
+            if step == 0:
+                nc.vector.tensor_copy(out=bias_col[:], in_=bias_ps[:, 0:M_TILES])
             if live(mid):
                 round_x4_on_vector(mid)
                 quantise(3, mid)
@@ -191,8 +191,6 @@ def tile_kanvolutionlayer_e_kernel(tc, x, Wp_words, Wp_scales, bp, Wq_words, Wq_
                 quantise(2, new)
             if live(done):
                 finish(done, 1)
-            if step == 0:
-                nc.vector.tensor_copy(out=bias_col[:], in_=bias_ps[:, 0:M_TILES])
             if live(new):
                 square_to_float32(x2_f32, "x2_f32", new, power[(1, new)])
             if live(old):

@@ -40,7 +40,7 @@ def tile_kanvolutionlayer_e_kernel(tc, x, Wp_words, Wp_scales, bp, Wq_words, Wq_
         powers = ctx.enter_context(tc.tile_pool(name="powers", bufs=3))
         scratch = ctx.enter_context(tc.tile_pool(name="scratch", bufs=2 * PAIRS))
         recips = ctx.enter_context(tc.tile_pool(name="recips", bufs=PAIRS * (FINISH_LAG - 1)))
-        results = ctx.enter_context(tc.tile_pool(name="results", bufs=4))
+        results = ctx.enter_context(tc.tile_pool(name="results", bufs=CHUNKS * PAIRS))
         q_banks = ctx.enter_context(tc.psum_pool(name="q_banks", bufs=PAIRS))
         p_banks = ctx.enter_context(tc.psum_pool(name="p_banks", bufs=PAIRS * (FINISH_LAG - 1)))
 
@@ -151,18 +151,20 @@ def tile_kanvolutionlayer_e_kernel(tc, x, Wp_words, Wp_scales, bp, Wq_words, Wq_
             nc.scalar.activation(out=recip[(c, pair)][:], in_=rsqrt[(c, pair)][:], func=ACT.Square)
 
         def finish(c, pair):
+            res = results.tile([P, 2, PIXELS], F32, name="res")
             for j in range(2):
                 m = 2 * pair + j
-                res = results.tile([P, PIXELS], F32, name="res")
                 nc.vector.scalar_tensor_tensor(
-                    out=res[:],
+                    out=res[:, j, :],
                     in0=sum_p[(c, pair)][:, j, :],
                     scalar=bias_col[:, m : m + 1],
                     in1=recip[(c, pair)][:, j, :],
                     op0=ALU.add,
                     op1=ALU.mult,
                 )
-                nc.sync.dma_start(out=out[c, m * P : (m + 1) * P].rearrange("o h w -> o (h w)"), in_=res[:])
+            nc.sync.dma_start(
+                out=out[c, 2 * pair * P : 2 * (pair + 1) * P].rearrange("(j o) h w -> o j (h w)", j=2), in_=res[:]
+            )
 
         def live(c):
             return 0 <= c < CHUNKS
@@ -173,8 +175,6 @@ def tile_kanvolutionlayer_e_kernel(tc, x, Wp_words, Wp_scales, bp, Wq_words, Wq_
                 times_x(3, mid, x2_f32[mid])
             if live(new):
                 regroup_x(new)
-            if step == 0:
-                nc.vector.tensor_copy(out=bias_col[:], in_=bias_ps[:, 0:M_TILES])
             if live(mid):
                 round_x4_on_vector(mid)
                 quantise(3, mid)
@@ -191,6 +191,8 @@ def tile_kanvolutionlayer_e_kernel(tc, x, Wp_words, Wp_scales, bp, Wq_words, Wq_
                 quantise(2, new)
             if live(done):
                 finish(done, 1)
+            if step == 0:
+                nc.vector.tensor_copy(out=bias_col[:], in_=bias_ps[:, 0:M_TILES])
             if live(new):
                 square_to_float32(x2_f32, "x2_f32", new, power[(1, new)])
             if live(old):

@@ -79,47 +79,58 @@ def tile_kanvolutionlayer_e_kernel(tc, x, Wp_words, Wp_scales, bp, Wq_words, Wq_
         nc.tensor.transpose(bias_ps[:], bias_rows[:], ident[:])
         bias_col = keep.tile([P, M_TILES], F32, name="bias_col")
 
-        codes = keep.tile([P, ORDERS_P, CHUNKS * PIXELS], U32, name="codes", align_bytes=64)
-        x_planes = keep.tile([P, ORDERS_P, CHUNKS * PIXELS], U8, name="x_planes", align_bytes=64)
+        codes = keep.tile([P, CHUNKS * ORDERS_P * PIXELS], U32, name="codes", align_bytes=64)
+        x_planes = keep.tile([P, CHUNKS * ORDERS_P * PIXELS], U8, name="x_planes", align_bytes=64)
+        pair_tile = {}
         power = {}
         x2_f32, x4_f32 = {}, {}
         sum_q, sum_p, rsqrt, recip = {}, {}, {}, {}
 
+        def columns(c, order, count=1):
+            first = (c * ORDERS_P + order - 1) * PIXELS
+            return slice(first, first + count * PIXELS)
+
         def new_power(order, c):
-            power[(order, c)] = powers.tile([P, WIDTH], BF16, name="x%d" % order, align_bytes=64)
+            if order == 5:
+                power[(order, c)] = powers.tile([P, WIDTH], BF16, name="x5", align_bytes=64)[:]
+                return power[(order, c)]
+            first = order - (order - 1) % 2
+            if (first, c) not in pair_tile:
+                pair_tile[(first, c)] = powers.tile([P, 2 * WIDTH], BF16, name="x%d%d" % (first, first + 1), align_bytes=64)
+            half = order - first
+            power[(order, c)] = pair_tile[(first, c)][:, half * WIDTH : (half + 1) * WIDTH]
             return power[(order, c)]
 
-        def quantise(order, c):
-            cols = slice(c * PIXELS, (c + 1) * PIXELS)
+        def quantise(order, c, count=1):
+            source = power[(order, c)] if count == 1 else pair_tile[(order, c)][:]
             nc.vector.quantize_mx(
-                out=codes[:, order - 1, cols].bitcast(FP8X4),
-                scales=x_planes[:, order - 1, cols],
-                in_=power[(order, c)][:],
+                out=codes[:, columns(c, order, count)].bitcast(FP8X4),
+                scales=x_planes[:, columns(c, order, count)],
+                in_=source,
             )
 
         def regroup_x(c):
             nc.vector.tensor_copy(
-                out=new_power(1, c)[:].rearrange("p (g i t) -> p g t i", i=RUN, t=PACK),
+                out=new_power(1, c).rearrange("p (g i t) -> p g t i", i=RUN, t=PACK),
                 in_=x_raw[:, c, :].rearrange("p (t g i) -> p g t i", t=PACK, i=RUN),
             )
 
         def times_x(order, c, lower_power):
-            nc.vector.tensor_tensor(out=new_power(order, c)[:], in0=lower_power[:], in1=power[(1, c)][:], op=ALU.mult)
+            nc.vector.tensor_tensor(out=new_power(order, c), in0=lower_power, in1=power[(1, c)], op=ALU.mult)
 
         def round_x4_on_vector(c):
             if c >= SCALAR_ROUNDS_X4:
-                nc.vector.tensor_copy(out=new_power(4, c)[:], in_=x4_f32[c][:])
+                nc.vector.tensor_copy(out=new_power(4, c), in_=x4_f32[c])
 
         def square_to_float32(squares, name, c, values):
-            squares[c] = powers.tile([P, WIDTH], F32, name=name)
-            nc.scalar.activation(out=squares[c][:], in_=values[:], func=ACT.Square)
+            squares[c] = powers.tile([P, WIDTH], F32, name=name)[:]
+            nc.scalar.activation(out=squares[c], in_=values, func=ACT.Square)
 
         def round_x4_on_scalar(c):
             if c < SCALAR_ROUNDS_X4:
-                nc.scalar.activation(out=new_power(4, c)[:], in_=x2_f32[c][:], func=ACT.Square)
+                nc.scalar.activation(out=new_power(4, c), in_=x2_f32[c], func=ACT.Square)
 
         def contract(c, sums, banks, tag, words, planes, orders):
-            cols = slice(c * PIXELS, (c + 1) * PIXELS)
             for pair in range(PAIRS):
                 sums[(c, pair)] = banks.tile([P, 2, PIXELS], F32, name=tag, tag=tag)
                 for j in range(2):
@@ -129,8 +140,8 @@ def tile_kanvolutionlayer_e_kernel(tc, x, Wp_words, Wp_scales, bp, Wq_words, Wq_
                             out=sums[(c, pair)][:, j, :],
                             lhsT=words[:, g, m * PACK * P : (m + 1) * PACK * P].bitcast(FP8X4),
                             lhsT_scale=planes[:, g, m * P : (m + 1) * P],
-                            rhs=codes[:, g, cols].bitcast(FP8X4),
-                            rhs_scale=x_planes[:, g, cols],
+                            rhs=codes[:, columns(c, g + 1)].bitcast(FP8X4),
+                            rhs_scale=x_planes[:, columns(c, g + 1)],
                             start=(g == 0),
                             stop=(g == orders - 1),
                         )
@@ -173,12 +184,11 @@ def tile_kanvolutionlayer_e_kernel(tc, x, Wp_words, Wp_scales, bp, Wq_words, Wq_
             new, mid, old, done = step, step - 1, step - 2, step - FINISH_LAG
             if live(mid):
                 times_x(3, mid, x2_f32[mid])
+                round_x4_on_vector(mid)
             if live(new):
                 regroup_x(new)
             if live(mid):
-                round_x4_on_vector(mid)
-                quantise(3, mid)
-                quantise(4, mid)
+                quantise(3, mid, 2)
                 times_x(5, mid, x4_f32[mid])
             if live(new):
                 times_x(2, new, power[(1, new)])
@@ -187,8 +197,7 @@ def tile_kanvolutionlayer_e_kernel(tc, x, Wp_words, Wp_scales, bp, Wq_words, Wq_
             if live(mid):
                 quantise(5, mid)
             if live(new):
-                quantise(1, new)
-                quantise(2, new)
+                quantise(1, new, 2)
             if live(done):
                 finish(done, 1)
             if step == 0:

@@ -21,6 +21,8 @@ M_TILES = OUT_CH // P
 PAIRS = M_TILES // 2
 RUN = 4
 SCALAR_ROUNDS_X4 = CHUNKS // 2
+IDLE_N = 512
+IDLE_AT_START, IDLE_AFTER_X2, IDLE_AFTER_X3 = 10, 4, 4
 FINISH_LAG = 4
 
 FLOPS = 2 * CHUNKS * PIXELS * OUT_CH * CHANNELS * (ORDERS_P + ORDERS_Q)
@@ -75,9 +77,17 @@ def tile_kanvolutionlayer_e_kernel(tc, x, Wp_words, Wp_scales, bp, Wq_words, Wq_
 
         ident = keep.tile([P, P], BF16, name="ident")
         make_identity(nc, ident[:])
-        bias_ps = q_banks.tile([P, P], BF16, name="bias_ps", tag="sum_q")
-        nc.tensor.transpose(bias_ps[:], bias_rows[:], ident[:])
         bias_col = keep.tile([P, M_TILES], F32, name="bias_col")
+
+        idle_rhs = keep.tile([P, IDLE_N], BF16, name="idle_rhs")
+        nc.vector.memset(idle_rhs[:], 0.0)
+        idle_ps = p_banks.tile([P, IDLE_N], F32, name="idle_ps", tag="sum_p")
+
+        def keep_tensor_busy(count, values):
+            for i in range(count):
+                nc.tensor.matmul(idle_ps[:], lhsT=ident[:], rhs=values, start=True, stop=True)
+
+        keep_tensor_busy(IDLE_AT_START, idle_rhs[:])
 
         codes = keep.tile([P, CHUNKS * ORDERS_P * PIXELS], U32, name="codes", align_bytes=64)
         x_planes = keep.tile([P, CHUNKS * ORDERS_P * PIXELS], U8, name="x_planes", align_bytes=64)
@@ -200,7 +210,7 @@ def tile_kanvolutionlayer_e_kernel(tc, x, Wp_words, Wp_scales, bp, Wq_words, Wq_
                 quantise(1, new, 2)
             if live(done):
                 finish(done, 1)
-            if step == 0:
+            if step == 2:
                 nc.vector.tensor_copy(out=bias_col[:], in_=bias_ps[:, 0:M_TILES])
             if live(new):
                 square_to_float32(x2_f32, "x2_f32", new, power[(1, new)])
@@ -212,6 +222,12 @@ def tile_kanvolutionlayer_e_kernel(tc, x, Wp_words, Wp_scales, bp, Wq_words, Wq_
                 reciprocal(old, 1)
             if live(new):
                 round_x4_on_scalar(new)
+            if step == 0:
+                keep_tensor_busy(IDLE_AFTER_X2, power[(2, 0)][:, 0:IDLE_N])
+            if step == 1:
+                keep_tensor_busy(IDLE_AFTER_X3, power[(3, 0)][:, 0:IDLE_N])
+                bias_ps = p_banks.tile([P, P], BF16, name="bias_ps", tag="sum_p")
+                nc.tensor.transpose(bias_ps[:], bias_rows[:], ident[:])
             if live(mid):
                 contract(mid, sum_q, q_banks, "sum_q", words_q, planes_q, ORDERS_Q)
                 contract(mid, sum_p, p_banks, "sum_p", words_p, planes_p, ORDERS_P)

@@ -63,12 +63,12 @@ def tile_kanvolutionlayer_e_kernel(tc, x, Wp_words, Wp_scales, bp, Wq_words, Wq_
         nc.vector.memset(one[:], 1.0)
 
         load_x(nc.sync, 0)
+        load_scale_planes(nc, planes_q, Wq_scales)
         load_x(nc.sync, 1)
         nc.scalar.dma_start(out=bias_rows[0:M_TILES, :], in_=bp.rearrange("(m p) -> m p", p=P))
         nc.sync.dma_start(out=words_q[:].bitcast(I32), in_=Wq_words.rearrange("g p n t -> p g (n t)").bitcast(I32))
-        load_scale_planes(nc, planes_q, Wq_scales)
-        load_scale_planes(nc, planes_p, Wp_scales)
         load_x(nc.sync, 2)
+        load_scale_planes(nc, planes_p, Wp_scales)
         nc.sync.dma_start(out=words_p[:].bitcast(I32), in_=Wp_words.rearrange("g p n t -> p g (n t)").bitcast(I32))
         load_x(nc.sync, 3)
 

@@ -167,9 +167,16 @@ def tile_kanvolutionlayer_e_kernel(tc, x, Wp_words, Wp_scales, bp, Wq_words, Wq_
                     out=rsqrt[(c, pair)][:], in_=mag[pair][:], func=ACT.Abs_reciprocal_sqrt, bias=1.0
                 )
 
+        def last_of_all(c, pair):
+            return c == CHUNKS - 1 and pair == PAIRS - 1
+
         def reciprocal(c, pair):
             recip[(c, pair)] = recips.tile([P, 2, PIXELS], F32, name="recip")
-            nc.scalar.activation(out=recip[(c, pair)][:], in_=rsqrt[(c, pair)][:], func=ACT.Square)
+            if last_of_all(c, pair):
+                for j in range(2):
+                    nc.scalar.activation(out=recip[(c, pair)][:, j, :], in_=rsqrt[(c, pair)][:, j, :], func=ACT.Square)
+            else:
+                nc.scalar.activation(out=recip[(c, pair)][:], in_=rsqrt[(c, pair)][:], func=ACT.Square)
 
         def finish(c, pair):
             res = results.tile([P, 2, PIXELS], F32, name="res")
@@ -183,9 +190,12 @@ def tile_kanvolutionlayer_e_kernel(tc, x, Wp_words, Wp_scales, bp, Wq_words, Wq_
                     op0=ALU.add,
                     op1=ALU.mult,
                 )
-            nc.sync.dma_start(
-                out=out[c, 2 * pair * P : 2 * (pair + 1) * P].rearrange("(j o) h w -> o j (h w)", j=2), in_=res[:]
-            )
+                if last_of_all(c, pair):
+                    nc.sync.dma_start(out=out[c, m * P : (m + 1) * P].rearrange("o h w -> o (h w)"), in_=res[:, j, :])
+            if not last_of_all(c, pair):
+                nc.sync.dma_start(
+                    out=out[c, 2 * pair * P : 2 * (pair + 1) * P].rearrange("(j o) h w -> o j (h w)", j=2), in_=res[:]
+                )
 
         def live(c):
             return 0 <= c < CHUNKS

@@ -22,7 +22,7 @@ PAIRS = M_TILES // 2
 RUN = 4
 SCALAR_ROUNDS_X4 = CHUNKS // 2
 IDLE_N = 512
-IDLE_AT_START, IDLE_AFTER_X2, IDLE_AFTER_X3 = 10, 4, 4
+IDLE_AT_START, IDLE_AFTER_X2, IDLE_AFTER_X3 = 6, 4, 4
 FINISH_LAG = 4
 
 FLOPS = 2 * CHUNKS * PIXELS * OUT_CH * CHANNELS * (ORDERS_P + ORDERS_Q)
@@ -57,10 +57,10 @@ def tile_kanvolutionlayer_e_kernel(tc, x, Wp_words, Wp_scales, bp, Wq_words, Wq_
         planes_p = keep.tile([P, ORDERS_P, OUT_CH], U8, name="planes_p", align_bytes=64)
         bias_rows = keep.tile([P, P], BF16, name="bias_rows")
         one = keep.tile([P, 1], F32, name="one")
-        nc.vector.memset(planes_q[:].bitcast(I32), 0)
-        nc.vector.memset(planes_p[:].bitcast(I32), 0)
         nc.vector.memset(bias_rows[:], 0.0)
         nc.vector.memset(one[:], 1.0)
+        nc.vector.memset(planes_q[:].bitcast(I32), 0)
+        nc.vector.memset(planes_p[:].bitcast(I32), 0)
 
         load_x(nc.sync, 0)
         load_scale_planes(nc, planes_q, Wq_scales)
@@ -227,11 +227,10 @@ def tile_kanvolutionlayer_e_kernel(tc, x, Wp_words, Wp_scales, bp, Wq_words, Wq_
             if live(old):
                 reciprocal(old, 0)
             if live(new):
+                round_x4_on_scalar(new)
                 square_to_float32(x4_f32, "x4_f32", new, x2_f32[new])
             if live(old):
                 reciprocal(old, 1)
-            if live(new):
-                round_x4_on_scalar(new)
             if step == 0:
                 keep_tensor_busy(IDLE_AFTER_X2, power[(2, 0)][:, 0:IDLE_N])
             if step == 1:

@@ -67,9 +67,9 @@ def tile_kanvolutionlayer_e_kernel(tc, x, Wp_words, Wp_scales, bp, Wq_words, Wq_
         load_x(nc.sync, 1)
         nc.scalar.dma_start(out=bias_rows[0:M_TILES, :], in_=bp.rearrange("(m p) -> m p", p=P))
         nc.sync.dma_start(out=words_q[:].bitcast(I32), in_=Wq_words.rearrange("g p n t -> p g (n t)").bitcast(I32))
-        load_x(nc.sync, 2)
         load_scale_planes(nc, planes_p, Wp_scales)
         nc.sync.dma_start(out=words_p[:].bitcast(I32), in_=Wp_words.rearrange("g p n t -> p g (n t)").bitcast(I32))
+        load_x(nc.sync, 2)
         load_x(nc.sync, 3)
 
         warm = keep.tile([P, 1], F32, name="warm")

@@ -23,6 +23,7 @@ RUN = 4
 SCALAR_ROUNDS_X4 = CHUNKS // 2
 IDLE_N = 512
 IDLE_AT_START, IDLE_AFTER_X2, IDLE_AFTER_X3 = 6, 4, 4
+LAST = CHUNKS - 1
 FINISH_LAG = 4
 
 FLOPS = 2 * CHUNKS * PIXELS * OUT_CH * CHANNELS * (ORDERS_P + ORDERS_Q)
@@ -94,7 +95,7 @@ def tile_kanvolutionlayer_e_kernel(tc, x, Wp_words, Wp_scales, bp, Wq_words, Wq_
         pair_tile = {}
         power = {}
         x2_f32, x4_f32 = {}, {}
-        sum_q, sum_p, rsqrt, recip = {}, {}, {}, {}
+        sum_q, sum_p, mag, rsqrt, recip = {}, {}, {}, {}, {}
 
         def columns(c, order, count=1):
             first = (c * ORDERS_P + order - 1) * PIXELS
@@ -156,16 +157,15 @@ def tile_kanvolutionlayer_e_kernel(tc, x, Wp_words, Wp_scales, bp, Wq_words, Wq_
                             stop=(g == orders - 1),
                         )
 
-        def reciprocal_roots(c):
-            mag = {}
-            for pair in range(PAIRS):
-                mag[pair] = scratch.tile([P, 2, PIXELS], F32, name="mag")
-                nc.scalar.activation(out=mag[pair][:], in_=sum_q[(c, pair)][:], func=ACT.Abs)
-            for pair in range(PAIRS):
-                rsqrt[(c, pair)] = scratch.tile([P, 2, PIXELS], F32, name="rsqrt")
-                nc.scalar.activation(
-                    out=rsqrt[(c, pair)][:], in_=mag[pair][:], func=ACT.Abs_reciprocal_sqrt, bias=1.0
-                )
+        def magnitude(c, pair):
+            mag[(c, pair)] = scratch.tile([P, 2, PIXELS], F32, name="mag")
+            nc.scalar.activation(out=mag[(c, pair)][:], in_=sum_q[(c, pair)][:], func=ACT.Abs)
+
+        def reciprocal_root(c, pair):
+            rsqrt[(c, pair)] = scratch.tile([P, 2, PIXELS], F32, name="rsqrt")
+            nc.scalar.activation(
+                out=rsqrt[(c, pair)][:], in_=mag[(c, pair)][:], func=ACT.Abs_reciprocal_sqrt, bias=1.0
+            )
 
         def last_of_all(c, pair):
             return c == CHUNKS - 1 and pair == PAIRS - 1
@@ -224,12 +224,12 @@ def tile_kanvolutionlayer_e_kernel(tc, x, Wp_words, Wp_scales, bp, Wq_words, Wq_
                 nc.vector.tensor_copy(out=bias_col[:], in_=bias_ps[:, 0:M_TILES])
             if live(new):
                 square_to_float32(x2_f32, "x2_f32", new, power[(1, new)])
-            if live(old):
+            if live(old) and old < LAST - 1:
                 reciprocal(old, 0)
             if live(new):
                 round_x4_on_scalar(new)
                 square_to_float32(x4_f32, "x4_f32", new, x2_f32[new])
-            if live(old):
+            if live(old) and old < LAST - 1:
                 reciprocal(old, 1)
             if step == 0:
                 keep_tensor_busy(IDLE_AFTER_X2, power[(2, 0)][:, 0:IDLE_N])
@@ -240,4 +240,17 @@ def tile_kanvolutionlayer_e_kernel(tc, x, Wp_words, Wp_scales, bp, Wq_words, Wq_
             if live(mid):
                 contract(mid, sum_q, q_banks, "sum_q", words_q, planes_q, ORDERS_Q)
                 contract(mid, sum_p, p_banks, "sum_p", words_p, planes_p, ORDERS_P)
-                reciprocal_roots(mid)
+                if mid < LAST:
+                    magnitude(mid, 0)
+                    magnitude(mid, 1)
+                    reciprocal_root(mid, 0)
+                    reciprocal_root(mid, 1)
+                else:
+                    reciprocal(mid - 1, 0)
+                    magnitude(mid, 0)
+                    reciprocal(mid - 1, 1)
+                    reciprocal_root(mid, 0)
+                    magnitude(mid, 1)
+                    reciprocal(mid, 0)
+                    reciprocal_root(mid, 1)
+                    reciprocal(mid, 1)

@@ -16,23 +16,24 @@ P = 128
 PACK = 4
 CHUNKS, CHANNELS, PIXELS, OUT_CH = 4, 512, 256, 512
 ORDERS_P, ORDERS_Q = 5, 4
+FIRST_Q, FIRST_P = 0, 4
 WIDTH = PIXELS * PACK
 M_TILES = OUT_CH // P
 PAIRS = M_TILES // 2
 RUN = 4
 SCALAR_ROUNDS_X4 = CHUNKS // 2
 IDLE_N = 512
-IDLE_AT_START, IDLE_AFTER_X2, IDLE_AFTER_X3 = 6, 4, 4
+IDLE_AT_START, IDLE_AFTER_X2, IDLE_AFTER_X3 = 4, 4, 4
 LAST = CHUNKS - 1
 FINISH_LAG = 4
 
 FLOPS = 2 * CHUNKS * PIXELS * OUT_CH * CHANNELS * (ORDERS_P + ORDERS_Q)
 
 
-def load_scale_planes(nc, planes, scales_in):
+def load_scale_planes(nc, planes, scales_in, first):
     by_row = scales_in.rearrange("g (quad r) n -> r quad g n", r=4)
     for r in range(4):
-        nc.sync.dma_start(out=planes[r:P:32, :, :].bitcast(I32), in_=by_row[r].bitcast(I32))
+        nc.sync.dma_start(out=planes[first + r : P : 32, :, :].bitcast(I32), in_=by_row[r].bitcast(I32))
 
 
 def tile_kanvolutionlayer_e_kernel(tc, x, Wp_words, Wp_scales, bp, Wq_words, Wq_scales, out):
@@ -64,11 +65,11 @@ def tile_kanvolutionlayer_e_kernel(tc, x, Wp_words, Wp_scales, bp, Wq_words, Wq_
         nc.vector.memset(planes_p[:].bitcast(I32), 0)
 
         load_x(nc.sync, 0)
-        load_scale_planes(nc, planes_q, Wq_scales)
+        load_scale_planes(nc, planes_q, Wq_scales, FIRST_Q)
         load_x(nc.sync, 1)
         nc.scalar.dma_start(out=bias_rows[0:M_TILES, :], in_=bp.rearrange("(m p) -> m p", p=P))
         nc.sync.dma_start(out=words_q[:].bitcast(I32), in_=Wq_words.rearrange("g p n t -> p g (n t)").bitcast(I32))
-        load_scale_planes(nc, planes_p, Wp_scales)
+        load_scale_planes(nc, planes_p, Wp_scales, FIRST_P)
         nc.sync.dma_start(out=words_p[:].bitcast(I32), in_=Wp_words.rearrange("g p n t -> p g (n t)").bitcast(I32))
         load_x(nc.sync, 2)
         load_x(nc.sync, 3)
@@ -135,13 +136,14 @@ def tile_kanvolutionlayer_e_kernel(tc, x, Wp_words, Wp_scales, bp, Wq_words, Wq_
 
         def square_to_float32(squares, name, c, values):
             squares[c] = powers.tile([P, WIDTH], F32, name=name)[:]
-            nc.scalar.activation(out=squares[c], in_=values, func=ACT.Square)
+            shaped = squares[c] if values.ndim == 2 else squares[c].rearrange("p (n t) -> p n t", t=PACK)
+            nc.scalar.activation(out=shaped, in_=values, func=ACT.Square)
 
         def round_x4_on_scalar(c):
             if c < SCALAR_ROUNDS_X4:
                 nc.scalar.activation(out=new_power(4, c), in_=x2_f32[c], func=ACT.Square)
 
-        def contract(c, sums, banks, tag, words, planes, orders):
+        def contract(c, sums, banks, tag, words, planes, first, orders):
             for pair in range(PAIRS):
                 sums[(c, pair)] = banks.tile([P, 2, PIXELS], F32, name=tag, tag=tag)
                 for j in range(2):
@@ -150,7 +152,7 @@ def tile_kanvolutionlayer_e_kernel(tc, x, Wp_words, Wp_scales, bp, Wq_words, Wq_
                         nc.tensor.matmul_mx(
                             out=sums[(c, pair)][:, j, :],
                             lhsT=words[:, g, m * PACK * P : (m + 1) * PACK * P].bitcast(FP8X4),
-                            lhsT_scale=planes[:, g, m * P : (m + 1) * P],
+                            lhsT_scale=planes[first:P, g, m * P : (m + 1) * P],
                             rhs=codes[:, columns(c, g + 1)].bitcast(FP8X4),
                             rhs_scale=x_planes[:, columns(c, g + 1)],
                             start=(g == 0),
@@ -202,8 +204,11 @@ def tile_kanvolutionlayer_e_kernel(tc, x, Wp_words, Wp_scales, bp, Wq_words, Wq_
 
         for step in range(CHUNKS + FINISH_LAG):
             new, mid, old, done = step, step - 1, step - 2, step - FINISH_LAG
+            if new == 0:
+                square_to_float32(x2_f32, "x2_f32", new, x_raw[:, new, :].rearrange("p (t n) -> p n t", t=PACK))
             if live(mid):
-                times_x(3, mid, x2_f32[mid])
+                if mid > 0:
+                    times_x(3, mid, x2_f32[mid])
                 round_x4_on_vector(mid)
             if live(new):
                 regroup_x(new)
@@ -216,13 +221,15 @@ def tile_kanvolutionlayer_e_kernel(tc, x, Wp_words, Wp_scales, bp, Wq_words, Wq_
                 finish(done, 0)
             if live(mid):
                 quantise(5, mid)
+            if new == 0:
+                times_x(3, new, x2_f32[new])
             if live(new):
                 quantise(1, new, 2)
             if live(done):
                 finish(done, 1)
             if step == 2:
                 nc.vector.tensor_copy(out=bias_col[:], in_=bias_ps[:, 0:M_TILES])
-            if live(new):
+            if live(new) and new > 0:
                 square_to_float32(x2_f32, "x2_f32", new, power[(1, new)])
             if live(old) and old < LAST - 1:
                 reciprocal(old, 0)
@@ -238,8 +245,8 @@ def tile_kanvolutionlayer_e_kernel(tc, x, Wp_words, Wp_scales, bp, Wq_words, Wq_
                 bias_ps = p_banks.tile([P, P], BF16, name="bias_ps", tag="sum_p")
                 nc.tensor.transpose(bias_ps[:], bias_rows[:], ident[:])
             if live(mid):
-                contract(mid, sum_q, q_banks, "sum_q", words_q, planes_q, ORDERS_Q)
-                contract(mid, sum_p, p_banks, "sum_p", words_p, planes_p, ORDERS_P)
+                contract(mid, sum_q, q_banks, "sum_q", words_q, planes_q, FIRST_Q, ORDERS_Q)
+                contract(mid, sum_p, p_banks, "sum_p", words_p, planes_p, FIRST_P, ORDERS_P)
                 if mid < LAST:
                     magnitude(mid, 0)
                     magnitude(mid, 1)

@@ -25,6 +25,7 @@ SCALAR_ROUNDS_X4 = CHUNKS // 2
 IDLE_N = 512
 IDLE_AT_START, IDLE_AFTER_X2, IDLE_AFTER_X3 = 4, 4, 4
 LAST = CHUNKS - 1
+EARLY_CHUNK, EARLY_ORDERS = 1, 2
 FINISH_LAG = 4
 
 FLOPS = 2 * CHUNKS * PIXELS * OUT_CH * CHANNELS * (ORDERS_P + ORDERS_Q)
@@ -143,21 +144,34 @@ def tile_kanvolutionlayer_e_kernel(tc, x, Wp_words, Wp_scales, bp, Wq_words, Wq_
             if c < SCALAR_ROUNDS_X4:
                 nc.scalar.activation(out=new_power(4, c), in_=x2_f32[c], func=ACT.Square)
 
+        def passes(c, sums, words, planes, first, orders, m, some_orders):
+            for g in some_orders:
+                nc.tensor.matmul_mx(
+                    out=sums[(c, m // 2)][:, m % 2, :],
+                    lhsT=words[:, g, m * PACK * P : (m + 1) * PACK * P].bitcast(FP8X4),
+                    lhsT_scale=planes[first:P, g, m * P : (m + 1) * P],
+                    rhs=codes[:, columns(c, g + 1)].bitcast(FP8X4),
+                    rhs_scale=x_planes[:, columns(c, g + 1)],
+                    start=(g == 0),
+                    stop=(g == orders - 1),
+                )
+
         def contract(c, sums, banks, tag, words, planes, first, orders):
             for pair in range(PAIRS):
                 sums[(c, pair)] = banks.tile([P, 2, PIXELS], F32, name=tag, tag=tag)
                 for j in range(2):
-                    m = 2 * pair + j
-                    for g in range(orders):
-                        nc.tensor.matmul_mx(
-                            out=sums[(c, pair)][:, j, :],
-                            lhsT=words[:, g, m * PACK * P : (m + 1) * PACK * P].bitcast(FP8X4),
-                            lhsT_scale=planes[first:P, g, m * P : (m + 1) * P],
-                            rhs=codes[:, columns(c, g + 1)].bitcast(FP8X4),
-                            rhs_scale=x_planes[:, columns(c, g + 1)],
-                            start=(g == 0),
-                            stop=(g == orders - 1),
-                        )
+                    passes(c, sums, words, planes, first, orders, 2 * pair + j, range(orders))
+
+        def open_sum_q(c):
+            for pair in range(PAIRS):
+                sum_q[(c, pair)] = p_banks.tile([P, 2, PIXELS], F32, name="sum_q_early", tag="sum_p")
+            for pair in range(PAIRS):
+                passes(c, sum_q, words_q, planes_q, FIRST_Q, ORDERS_Q, 2 * pair, range(EARLY_ORDERS))
+
+        def close_sum_q(c):
+            for pair in range(PAIRS):
+                passes(c, sum_q, words_q, planes_q, FIRST_Q, ORDERS_Q, 2 * pair, range(EARLY_ORDERS, ORDERS_Q))
+                passes(c, sum_q, words_q, planes_q, FIRST_Q, ORDERS_Q, 2 * pair + 1, range(ORDERS_Q))
 
         def magnitude(c, pair):
             mag[(c, pair)] = scratch.tile([P, 2, PIXELS], F32, name="mag")
@@ -206,29 +220,37 @@ def tile_kanvolutionlayer_e_kernel(tc, x, Wp_words, Wp_scales, bp, Wq_words, Wq_
             new, mid, old, done = step, step - 1, step - 2, step - FINISH_LAG
             if new == 0:
                 square_to_float32(x2_f32, "x2_f32", new, x_raw[:, new, :].rearrange("p (t n) -> p n t", t=PACK))
+            if step == 2:
+                nc.vector.tensor_copy(out=bias_col[:], in_=bias_ps[:, 0:M_TILES])
             if live(mid):
                 if mid > 0:
                     times_x(3, mid, x2_f32[mid])
                 round_x4_on_vector(mid)
-            if live(new):
+            if live(new) and new != 1:
                 regroup_x(new)
-            if live(mid):
+            if new == EARLY_CHUNK:
                 quantise(3, mid, 2)
-                times_x(5, mid, x4_f32[mid])
-            if live(new):
                 times_x(2, new, power[(1, new)])
-            if live(done):
-                finish(done, 0)
-            if live(mid):
-                quantise(5, mid)
-            if new == 0:
-                times_x(3, new, x2_f32[new])
-            if live(new):
+                times_x(5, mid, x4_f32[mid])
                 quantise(1, new, 2)
-            if live(done):
-                finish(done, 1)
-            if step == 2:
-                nc.vector.tensor_copy(out=bias_col[:], in_=bias_ps[:, 0:M_TILES])
+                quantise(5, mid)
+            else:
+                if live(mid):
+                    quantise(3, mid, 2)
+                    times_x(5, mid, x4_f32[mid])
+                if live(new):
+                    times_x(2, new, power[(1, new)])
+                if live(done):
+                    finish(done, 0)
+                if live(mid):
+                    quantise(5, mid)
+                if new == 0:
+                    times_x(3, new, x2_f32[new])
+                    regroup_x(new + 1)
+                if live(new):
+                    quantise(1, new, 2)
+                if live(done):
+                    finish(done, 1)
             if live(new) and new > 0:
                 square_to_float32(x2_f32, "x2_f32", new, power[(1, new)])
             if live(old) and old < LAST - 1:
@@ -245,7 +267,12 @@ def tile_kanvolutionlayer_e_kernel(tc, x, Wp_words, Wp_scales, bp, Wq_words, Wq_
                 bias_ps = p_banks.tile([P, P], BF16, name="bias_ps", tag="sum_p")
                 nc.tensor.transpose(bias_ps[:], bias_rows[:], ident[:])
             if live(mid):
-                contract(mid, sum_q, q_banks, "sum_q", words_q, planes_q, FIRST_Q, ORDERS_Q)
+                if mid == EARLY_CHUNK:
+                    close_sum_q(mid)
+                else:
+                    contract(mid, sum_q, q_banks, "sum_q", words_q, planes_q, FIRST_Q, ORDERS_Q)
+                if mid + 1 == EARLY_CHUNK:
+                    open_sum_q(mid + 1)
                 contract(mid, sum_p, p_banks, "sum_p", words_p, planes_p, FIRST_P, ORDERS_P)
                 if mid < LAST:
                     magnitude(mid, 0)

from contextlib import ExitStack

import concourse.mybir as mybir
from concourse.masks import make_identity

BF16 = mybir.dt.bfloat16
F32 = mybir.dt.float32
I32 = mybir.dt.int32
U32 = mybir.dt.uint32
U8 = mybir.dt.uint8
FP8X4 = mybir.dt.float8_e4m3fn_x4
ACT = mybir.ActivationFunctionType
ALU = mybir.AluOpType

P = 128
PACK = 4
CHUNKS, CHANNELS, PIXELS, OUT_CH = 4, 512, 256, 512
ORDERS_P, ORDERS_Q = 5, 4
FIRST_Q, FIRST_P = 0, 4
WIDTH = PIXELS * PACK
M_TILES = OUT_CH // P
PAIRS = M_TILES // 2
RUN = 4
SCALAR_ROUNDS_X4 = CHUNKS // 2
IDLE_N = 512
IDLE_AT_START, IDLE_AFTER_X2, IDLE_AFTER_X3 = 4, 4, 4
LAST = CHUNKS - 1
EARLY_CHUNK, EARLY_ORDERS = 1, 2
FINISH_LAG = 4

FLOPS = 2 * CHUNKS * PIXELS * OUT_CH * CHANNELS * (ORDERS_P + ORDERS_Q)


def load_scale_planes(nc, planes, scales_in, first):
    by_row = scales_in.rearrange("g (quad r) n -> r quad g n", r=4)
    for r in range(4):
        nc.sync.dma_start(out=planes[first + r : P : 32, :, :].bitcast(I32), in_=by_row[r].bitcast(I32))


def tile_kanvolutionlayer_e_kernel(tc, x, Wp_words, Wp_scales, bp, Wq_words, Wq_scales, out):
    nc = tc.nc
    with ExitStack() as ctx:
        ctx.enter_context(tc.manual_schedule())
        keep = ctx.enter_context(tc.tile_pool(name="keep", bufs=1))
        powers = ctx.enter_context(tc.tile_pool(name="powers", bufs=3))
        scratch = ctx.enter_context(tc.tile_pool(name="scratch", bufs=2 * PAIRS))
        recips = ctx.enter_context(tc.tile_pool(name="recips", bufs=PAIRS * (FINISH_LAG - 1)))
        results = ctx.enter_context(tc.tile_pool(name="results", bufs=CHUNKS * PAIRS))
        q_banks = ctx.enter_context(tc.psum_pool(name="q_banks", bufs=PAIRS))
        p_banks = ctx.enter_context(tc.psum_pool(name="p_banks", bufs=PAIRS * (FINISH_LAG - 1)))

        x_raw = keep.tile([P, CHUNKS, WIDTH], BF16, name="x_raw")

        def load_x(queue, c):
            queue.dma_start(out=x_raw[:, c, :], in_=x[c].rearrange("(p t) h w -> p (t h w)", t=PACK))

        words_q = keep.tile([P, ORDERS_Q, PACK * OUT_CH], U8, name="words_q", align_bytes=64)
        words_p = keep.tile([P, ORDERS_P, PACK * OUT_CH], U8, name="words_p", align_bytes=64)
        planes_q = keep.tile([P, ORDERS_Q, OUT_CH], U8, name="planes_q", align_bytes=64)
        planes_p = keep.tile([P, ORDERS_P, OUT_CH], U8, name="planes_p", align_bytes=64)
        bias_rows = keep.tile([P, P], BF16, name="bias_rows")
        one = keep.tile([P, 1], F32, name="one")
        nc.vector.memset(bias_rows[:], 0.0)
        nc.vector.memset(one[:], 1.0)
        nc.vector.memset(planes_q[:].bitcast(I32), 0)
        nc.vector.memset(planes_p[:].bitcast(I32), 0)

        load_x(nc.sync, 0)
        load_scale_planes(nc, planes_q, Wq_scales, FIRST_Q)
        load_x(nc.sync, 1)
        nc.scalar.dma_start(out=bias_rows[0:M_TILES, :], in_=bp.rearrange("(m p) -> m p", p=P))
        nc.sync.dma_start(out=words_q[:].bitcast(I32), in_=Wq_words.rearrange("g p n t -> p g (n t)").bitcast(I32))
        load_scale_planes(nc, planes_p, Wp_scales, FIRST_P)
        nc.sync.dma_start(out=words_p[:].bitcast(I32), in_=Wp_words.rearrange("g p n t -> p g (n t)").bitcast(I32))
        load_x(nc.sync, 2)
        load_x(nc.sync, 3)

        warm = keep.tile([P, 1], F32, name="warm")
        nc.scalar.activation(out=warm[:], in_=one[:], func=ACT.Abs_reciprocal_sqrt)

        ident = keep.tile([P, P], BF16, name="ident")
        make_identity(nc, ident[:])
        bias_col = keep.tile([P, M_TILES], F32, name="bias_col")

        idle_rhs = keep.tile([P, IDLE_N], BF16, name="idle_rhs")
        nc.vector.memset(idle_rhs[:], 0.0)
        idle_ps = p_banks.tile([P, IDLE_N], F32, name="idle_ps", tag="sum_p")

        def keep_tensor_busy(count, values):
            for i in range(count):
                nc.tensor.matmul(idle_ps[:], lhsT=ident[:], rhs=values, start=True, stop=True)

        keep_tensor_busy(IDLE_AT_START, idle_rhs[:])

        codes = keep.tile([P, CHUNKS * ORDERS_P * PIXELS], U32, name="codes", align_bytes=64)
        x_planes = keep.tile([P, CHUNKS * ORDERS_P * PIXELS], U8, name="x_planes", align_bytes=64)
        pair_tile = {}
        power = {}
        x2_f32, x4_f32 = {}, {}
        sum_q, sum_p, mag, rsqrt, recip = {}, {}, {}, {}, {}

        def columns(c, order, count=1):
            first = (c * ORDERS_P + order - 1) * PIXELS
            return slice(first, first + count * PIXELS)

        def new_power(order, c):
            if order == 5:
                power[(order, c)] = powers.tile([P, WIDTH], BF16, name="x5", align_bytes=64)[:]
                return power[(order, c)]
            first = order - (order - 1) % 2
            if (first, c) not in pair_tile:
                pair_tile[(first, c)] = powers.tile([P, 2 * WIDTH], BF16, name="x%d%d" % (first, first + 1), align_bytes=64)
            half = order - first
            power[(order, c)] = pair_tile[(first, c)][:, half * WIDTH : (half + 1) * WIDTH]
            return power[(order, c)]

        def quantise(order, c, count=1):
            source = power[(order, c)] if count == 1 else pair_tile[(order, c)][:]
            nc.vector.quantize_mx(
                out=codes[:, columns(c, order, count)].bitcast(FP8X4),
                scales=x_planes[:, columns(c, order, count)],
                in_=source,
            )

        def regroup_x(c):
            nc.vector.tensor_copy(
                out=new_power(1, c).rearrange("p (g i t) -> p g t i", i=RUN, t=PACK),
                in_=x_raw[:, c, :].rearrange("p (t g i) -> p g t i", t=PACK, i=RUN),
            )

        def times_x(order, c, lower_power):
            nc.vector.tensor_tensor(out=new_power(order, c), in0=lower_power, in1=power[(1, c)], op=ALU.mult)

        def round_x4_on_vector(c):
            if c >= SCALAR_ROUNDS_X4:
                nc.vector.tensor_copy(out=new_power(4, c), in_=x4_f32[c])

        def square_to_float32(squares, name, c, values):
            squares[c] = powers.tile([P, WIDTH], F32, name=name)[:]
            shaped = squares[c] if values.ndim == 2 else squares[c].rearrange("p (n t) -> p n t", t=PACK)
            nc.scalar.activation(out=shaped, in_=values, func=ACT.Square)

        def round_x4_on_scalar(c):
            if c < SCALAR_ROUNDS_X4:
                nc.scalar.activation(out=new_power(4, c), in_=x2_f32[c], func=ACT.Square)

        def passes(c, sums, words, planes, first, orders, m, some_orders):
            for g in some_orders:
                nc.tensor.matmul_mx(
                    out=sums[(c, m // 2)][:, m % 2, :],
                    lhsT=words[:, g, m * PACK * P : (m + 1) * PACK * P].bitcast(FP8X4),
                    lhsT_scale=planes[first:P, g, m * P : (m + 1) * P],
                    rhs=codes[:, columns(c, g + 1)].bitcast(FP8X4),
                    rhs_scale=x_planes[:, columns(c, g + 1)],
                    start=(g == 0),
                    stop=(g == orders - 1),
                )

        def contract(c, sums, banks, tag, words, planes, first, orders):
            for pair in range(PAIRS):
                sums[(c, pair)] = banks.tile([P, 2, PIXELS], F32, name=tag, tag=tag)
                for j in range(2):
                    passes(c, sums, words, planes, first, orders, 2 * pair + j, range(orders))

        def open_sum_q(c):
            for pair in range(PAIRS):
                sum_q[(c, pair)] = p_banks.tile([P, 2, PIXELS], F32, name="sum_q_early", tag="sum_p")
            for pair in range(PAIRS):
                passes(c, sum_q, words_q, planes_q, FIRST_Q, ORDERS_Q, 2 * pair, range(EARLY_ORDERS))

        def close_sum_q(c):
            for pair in range(PAIRS):
                passes(c, sum_q, words_q, planes_q, FIRST_Q, ORDERS_Q, 2 * pair, range(EARLY_ORDERS, ORDERS_Q))
                passes(c, sum_q, words_q, planes_q, FIRST_Q, ORDERS_Q, 2 * pair + 1, range(ORDERS_Q))

        def magnitude(c, pair):
            mag[(c, pair)] = scratch.tile([P, 2, PIXELS], F32, name="mag")
            nc.scalar.activation(out=mag[(c, pair)][:], in_=sum_q[(c, pair)][:], func=ACT.Abs)

        def reciprocal_root(c, pair):
            rsqrt[(c, pair)] = scratch.tile([P, 2, PIXELS], F32, name="rsqrt")
            nc.scalar.activation(
                out=rsqrt[(c, pair)][:], in_=mag[(c, pair)][:], func=ACT.Abs_reciprocal_sqrt, bias=1.0
            )

        def last_of_all(c, pair):
            return c == CHUNKS - 1 and pair == PAIRS - 1

        def reciprocal(c, pair):
            recip[(c, pair)] = recips.tile([P, 2, PIXELS], F32, name="recip")
            if last_of_all(c, pair):
                for j in range(2):
                    nc.scalar.activation(out=recip[(c, pair)][:, j, :], in_=rsqrt[(c, pair)][:, j, :], func=ACT.Square)
            else:
                nc.scalar.activation(out=recip[(c, pair)][:], in_=rsqrt[(c, pair)][:], func=ACT.Square)

        def finish(c, pair):
            res = results.tile([P, 2, PIXELS], F32, name="res")
            for j in range(2):
                m = 2 * pair + j
                nc.vector.scalar_tensor_tensor(
                    out=res[:, j, :],
                    in0=sum_p[(c, pair)][:, j, :],
                    scalar=bias_col[:, m : m + 1],
                    in1=recip[(c, pair)][:, j, :],
                    op0=ALU.add,
                    op1=ALU.mult,
                )
                if last_of_all(c, pair):
                    nc.sync.dma_start(out=out[c, m * P : (m + 1) * P].rearrange("o h w -> o (h w)"), in_=res[:, j, :])
            if not last_of_all(c, pair):
                nc.sync.dma_start(
                    out=out[c, 2 * pair * P : 2 * (pair + 1) * P].rearrange("(j o) h w -> o j (h w)", j=2), in_=res[:]
                )

        def live(c):
            return 0 <= c < CHUNKS

        for step in range(CHUNKS + FINISH_LAG):
            new, mid, old, done = step, step - 1, step - 2, step - FINISH_LAG
            if new == 0:
                square_to_float32(x2_f32, "x2_f32", new, x_raw[:, new, :].rearrange("p (t n) -> p n t", t=PACK))
            if step == 2:
                nc.vector.tensor_copy(out=bias_col[:], in_=bias_ps[:, 0:M_TILES])
            if live(mid):
                if mid > 0:
                    times_x(3, mid, x2_f32[mid])
                round_x4_on_vector(mid)
            if live(new) and new != 1:
                regroup_x(new)
            if new == EARLY_CHUNK:
                quantise(3, mid, 2)
                times_x(2, new, power[(1, new)])
                times_x(5, mid, x4_f32[mid])
                quantise(1, new, 2)
                quantise(5, mid)
            else:
                if live(mid):
                    quantise(3, mid, 2)
                    times_x(5, mid, x4_f32[mid])
                if live(new):
                    times_x(2, new, power[(1, new)])
                if live(done):
                    finish(done, 0)
                if live(mid):
                    quantise(5, mid)
                if new == 0:
                    times_x(3, new, x2_f32[new])
                    regroup_x(new + 1)
                if live(new):
                    quantise(1, new, 2)
                if live(done):
                    finish(done, 1)
            if live(new) and new > 0:
                square_to_float32(x2_f32, "x2_f32", new, power[(1, new)])
            if live(old) and old < LAST - 1:
                reciprocal(old, 0)
            if live(new):
                round_x4_on_scalar(new)
                square_to_float32(x4_f32, "x4_f32", new, x2_f32[new])
            if live(old) and old < LAST - 1:
                reciprocal(old, 1)
            if step == 0:
                keep_tensor_busy(IDLE_AFTER_X2, power[(2, 0)][:, 0:IDLE_N])
            if step == 1:
                keep_tensor_busy(IDLE_AFTER_X3, power[(3, 0)][:, 0:IDLE_N])
                bias_ps = p_banks.tile([P, P], BF16, name="bias_ps", tag="sum_p")
                nc.tensor.transpose(bias_ps[:], bias_rows[:], ident[:])
            if live(mid):
                if mid == EARLY_CHUNK:
                    close_sum_q(mid)
                else:
                    contract(mid, sum_q, q_banks, "sum_q", words_q, planes_q, FIRST_Q, ORDERS_Q)
                if mid + 1 == EARLY_CHUNK:
                    open_sum_q(mid + 1)
                contract(mid, sum_p, p_banks, "sum_p", words_p, planes_p, FIRST_P, ORDERS_P)
                if mid < LAST:
                    magnitude(mid, 0)
                    magnitude(mid, 1)
                    reciprocal_root(mid, 0)
                    reciprocal_root(mid, 1)
                else:
                    reciprocal(mid - 1, 0)
                    magnitude(mid, 0)
                    reciprocal(mid - 1, 1)
                    reciprocal_root(mid, 0)
                    magnitude(mid, 1)
                    reciprocal(mid, 0)
                    reciprocal_root(mid, 1)
                    reciprocal(mid, 1)
